import numpy as np
import ml_dtypes


def mxq(x, axis, fmt="e4m3"):
    dtype, down = {"e4m3": (ml_dtypes.float8_e4m3fn, 7), "e5m2": (ml_dtypes.float8_e5m2, 14)}[fmt]
    v = np.moveaxis(np.asarray(x, np.float32).astype(ml_dtypes.bfloat16).astype(np.float64), axis, -1)
    blocks = v.reshape(v.shape[:-1] + (-1, 32))
    amax = np.abs(blocks).max(-1, keepdims=True)
    byte = np.maximum(np.where(amax > 0, np.frexp(amax)[1] - 1 + 127, 0) - down, 1)
    scale = np.exp2(byte - 127.0)
    codes = (blocks / scale).astype(np.float32).astype(dtype).astype(np.float64)
    return np.moveaxis((codes * scale).reshape(v.shape), -1, axis)


WIDE = False


def mx_kscale(k):
    if not WIDE:
        return np.ones(k)
    levels = np.array([20, -20, 10, -10, 0])
    a = np.random.permutation(np.resize(levels, k // 512 * 4)).reshape(k // 512, 4)
    idx = np.arange(k)
    return np.exp2(a[idx // 512, idx % 128 // 32])


BF16 = ml_dtypes.bfloat16


def bf(x):
    return np.asarray(x, np.float32).astype(BF16)


def f64(x):
    return np.asarray(x).astype(np.float64)


B, I, O, ORDER = 2048, 512, 512, 8
LO, HI = -1.0, 1.0


def setup_inputs():
    j = np.arange(ORDER)
    binom = np.cumprod(np.concatenate(([1.0], (ORDER - j) / (j + 1.0))))
    u = mx_kscale(O)
    x = np.random.standard_normal((B, I))
    weights = np.random.standard_normal((O, I)) / u[:, None]
    coeffs = np.random.standard_normal((O, I, ORDER + 1)) * binom / (HI - LO) ** ORDER * 2.0 / np.sqrt(I)
    g = np.random.standard_normal((B, O)) * np.exp2(np.random.randint(-12, 1, (B, 1))) * 4.0 * u
    return {"x": bf(x), "weights": bf(weights), "coeffs": bf(coeffs), "grad_out": bf(g)}


def reference(x, weights, coeffs, grad_out):
    K = coeffs.shape[-1] - 1
    zoom = (HI - LO) / 2.0
    pan = (HI + LO) / 2.0
    th = np.tanh(f64(x))
    xt = th * zoom + pan
    x_a = (xt - LO)[..., None]
    x_b = (HI - xt)[..., None]
    e = np.arange(K + 1)
    dber = e * x_a ** np.maximum(e - 1, 0) * x_b ** (K - e) - (K - e) * x_a ** e * x_b ** np.maximum(K - e - 1, 0)
    dber = dber * (zoom * (1.0 - th * th))[..., None]
    wc = f64(coeffs) * f64(weights)[..., None]
    wk = wc.reshape(wc.shape[0], -1)
    G = mxq(f64(grad_out), 1, "e5m2") @ mxq(wk, 0, "e4m3")
    G = G.reshape(dber.shape)
    return (G * dber).sum(axis=-1)

@@ -1,0 +1,230 @@
+import math
+from contextlib import ExitStack
+
+import concourse.mybir as mybir
+from concourse.masks import make_identity
+
+F32 = mybir.dt.float32
+BF16 = mybir.dt.bfloat16
+U32 = mybir.dt.uint32
+U8 = mybir.dt.uint8
+E4M3_X4 = mybir.dt.float8_e4m3fn_x4
+E5M2_X4 = mybir.dt.float8_e5m2_x4
+ALU = mybir.AluOpType
+ACT = mybir.ActivationFunctionType
+
+P = 128
+PACK = 4
+TOKENS, FEATURES, OUTPUTS, ORDER = 2048, 512, 512, 8
+TERMS = ORDER + 1
+CHUNK = 512
+BLOCKS = CHUNK // P
+N_CHUNKS = TOKENS // CHUNK
+N_GROUPS = FEATURES // P
+X_LIMIT = 8.0
+
+FLOPS = 2 * TOKENS * OUTPUTS * FEATURES * TERMS
+
+
+def binomial(n, k):
+    value = 1
+    for j in range(k):
+        value = value * (n - j) // (j + 1)
+    return value
+
+
+def tile_custombernsteinlayer_kernel(tc, x, weights, coeffs, grad_out, out):
+    nc = tc.nc
+    with ExitStack() as ctx:
+        keep = ctx.enter_context(tc.tile_pool(name="keep", bufs=1))
+        stage = ctx.enter_context(tc.tile_pool(name="stage", bufs=2))
+        mx_psum = ctx.enter_context(tc.psum_pool(name="mx_psum", bufs=5))
+        tr_psum = ctx.enter_context(tc.psum_pool(name="tr_psum", bufs=2))
+        sum_psum = ctx.enter_context(tc.psum_pool(name="sum_psum", bufs=1))
+
+        ident_f32 = keep.tile([P, P], F32)
+        make_identity(nc, ident_f32[:])
+        ident_bf16 = keep.tile([P, P], BF16)
+        make_identity(nc, ident_bf16[:])
+
+        x_rows = keep.tile([P, N_CHUNKS * BLOCKS, FEATURES], BF16)
+        g_rows = keep.tile([P, N_CHUNKS * BLOCKS, OUTPUTS], BF16)
+        w_rows = keep.tile([P, 2, 2, FEATURES], BF16)
+        g_codes = keep.tile([P, TOKENS], U32, align_bytes=64)
+        g_scales = keep.tile([P, TOKENS], U8, align_bytes=64)
+        wc_codes = keep.tile([P, N_GROUPS, TERMS * P], U32, align_bytes=64)
+        wc_scales = keep.tile([P, N_GROUPS, TERMS * P], U8, align_bytes=64)
+
+        coeff_view = coeffs.rearrange("(u p e) i k -> p u e (i k)", u=2, e=2)
+        group_cols = P * TERMS
+
+        def load_coeffs(group):
+            co = stage.tile([P, 2, 2, group_cols], BF16, tag="co")
+            for u in range(2):
+                nc.sync.dma_start(
+                    out=co[:, u, :, :],
+                    in_=coeff_view[:, u, :, group * group_cols : (group + 1) * group_cols],
+                )
+            return co
+
+        def load_tokens(chunk):
+            rows = slice(chunk * CHUNK, (chunk + 1) * CHUNK)
+            blocks = slice(chunk * BLOCKS, (chunk + 1) * BLOCKS)
+            nc.sync.dma_start(out=g_rows[:, blocks, :], in_=grad_out[rows, :].rearrange("(b p) o -> p b o", p=P))
+            nc.sync.dma_start(out=x_rows[:, blocks, :], in_=x[rows, :].rearrange("(b p) i -> p b i", p=P))
+
+        nc.sync.dma_start(out=w_rows[:], in_=weights.rearrange("(u p e) i -> p u e i", u=2, e=2))
+        coeff_tiles = {0: load_coeffs(0)}
+        load_tokens(0)
+        load_tokens(1)
+        coeff_tiles[1] = load_coeffs(1)
+        load_tokens(2)
+        load_tokens(3)
+
+        def quantise_wc(group):
+            co = coeff_tiles[group]
+            wq = stage.tile([P, TERMS, P, PACK], BF16, tag="wq", bufs=1, align_bytes=64)
+            gains = w_rows[:, :, :, group * P : (group + 1) * P].rearrange("p u e i -> p i (u e)")
+            nc.vector.tensor_tensor(
+                out=wq[:],
+                in0=co[:].rearrange("p u e (i k) -> p k i (u e)", k=TERMS),
+                in1=gains.unsqueeze(1).to_broadcast([P, TERMS, P, PACK]),
+                op=ALU.mult,
+            )
+            flat = wq[:].rearrange("p k i t -> p (k i t)")
+            wide = ORDER * P
+            nc.vector.quantize_mx(
+                out=wc_codes[:, group, 0:wide].bitcast(E4M3_X4),
+                scales=wc_scales[:, group, 0:wide],
+                in_=flat[:, 0 : wide * PACK],
+            )
+            nc.vector.quantize_mx(
+                out=wc_codes[:, group, wide : wide + P].bitcast(E4M3_X4),
+                scales=wc_scales[:, group, wide : wide + P],
+                in_=flat[:, wide * PACK : (wide + P) * PACK],
+            )
+            if group + 2 < N_GROUPS:
+                coeff_tiles[group + 2] = load_coeffs(group + 2)
+
+        def quantise_grad(chunk):
+            g_words = g_rows[:].bitcast(F32)
+            gq = stage.tile([P, CHUNK * PACK], BF16, tag="gq", align_bytes=64)
+            gq_words = gq[:].bitcast(F32).rearrange("p (n u) -> p n u", u=2)
+            for half in range(2):
+                g_t = tr_psum.tile([P, 2, 2 * P], F32, tag="tr")
+                for b in range(2):
+                    block = chunk * BLOCKS + 2 * half + b
+                    for u in range(2):
+                        nc.tensor.transpose(
+                            out=g_t[:, u, b * P : (b + 1) * P],
+                            in_=g_words[:, block, u * P : (u + 1) * P],
+                            identity=ident_f32[:],
+                        )
+                nc.scalar.copy(
+                    out=gq_words[:, half * 2 * P : (half + 1) * 2 * P, :],
+                    in_=g_t[:].rearrange("p u n -> p n u"),
+                )
+            cols = slice(chunk * CHUNK, (chunk + 1) * CHUNK)
+            nc.vector.quantize_mx(out=g_codes[:, cols].bitcast(E5M2_X4), scales=g_scales[:, cols], in_=gq[:])
+            blocks = slice(chunk * BLOCKS, (chunk + 1) * BLOCKS)
+            nc.gpsimd.tensor_scalar(
+                out=x_rows[:, blocks, :], in0=x_rows[:, blocks, :],
+                scalar1=-X_LIMIT, scalar2=X_LIMIT, op0=ALU.max, op1=ALU.min,
+            )
+
+        def make_weights(group, chunk):
+            x_t = tr_psum.tile([P, CHUNK], BF16, tag="tr")
+            for b in range(BLOCKS):
+                nc.tensor.transpose(
+                    out=x_t[:, b * P : (b + 1) * P],
+                    in_=x_rows[:, chunk * BLOCKS + b, group * P : (group + 1) * P],
+                    identity=ident_bf16[:],
+                )
+            e_planes = stage.tile([P, ORDER, CHUNK], F32, tag="e_planes")
+            for j in range(ORDER):
+                nc.scalar.activation(
+                    out=e_planes[:, j, :], in_=x_t[:], func=ACT.Exp,
+                    scale=float(2 * j - 6), bias=math.log(binomial(ORDER - 1, j)),
+                )
+            d_planes = stage.tile([P, ORDER - 1, CHUNK], F32, tag="d_planes")
+            for k in range(1, ORDER):
+                nc.gpsimd.tensor_tensor(
+                    out=d_planes[:, k - 1, :], in0=e_planes[:, k - 1, :], in1=e_planes[:, k, :], op=ALU.subtract
+                )
+            x_part = x_rows[:, chunk * BLOCKS : (chunk + 1) * BLOCKS, group * P : (group + 1) * P]
+            t_part = stage.tile([P, BLOCKS, P], F32, tag="t_part", bufs=3)
+            c_part = stage.tile([P, BLOCKS, P], F32, tag="c_part", bufs=3)
+            nc.scalar.activation(out=t_part[:], in_=x_part, func=ACT.Tanh)
+            nc.scalar.activation(out=c_part[:], in_=t_part[:], func=ACT.Square)
+            nc.scalar.activation(out=c_part[:], in_=c_part[:], func=ACT.Square, scale=-1.0, bias=1.0)
+            nc.scalar.activation(out=c_part[:], in_=c_part[:], func=ACT.Square)
+            return e_planes, d_planes, t_part, c_part
+
+        def multiply(group, chunk, e_planes, d_planes):
+            products = stage.tile([P, TERMS, CHUNK], F32, tag="products")
+            cols = slice(chunk * CHUNK, (chunk + 1) * CHUNK)
+            for k in range(TERMS):
+                g_k = mx_psum.tile([P, CHUNK], F32, tag="g_k")
+                nc.tensor.matmul_mx(
+                    out=g_k[:],
+                    lhsT=wc_codes[:, group, k * P : (k + 1) * P].bitcast(E4M3_X4),
+                    lhsT_scale=wc_scales[:, group, k * P : (k + 1) * P],
+                    rhs=g_codes[:, cols].bitcast(E5M2_X4),
+                    rhs_scale=g_scales[:, cols],
+                    start=True,
+                    stop=True,
+                )
+                gamma = -8.0 / binomial(ORDER, k)
+                if k == 0:
+                    plane, factor = e_planes[:, 0, :], -gamma
+                elif k == ORDER:
+                    plane, factor = e_planes[:, ORDER - 1, :], gamma
+                else:
+                    plane, factor = d_planes[:, k - 1, :], gamma
+                nc.vector.scalar_tensor_tensor(
+                    out=products[:, k, :], in0=g_k[:], scalar=factor, in1=plane, op0=ALU.mult, op1=ALU.mult
+                )
+            return products
+
+        def sum_and_store(group, chunk, products, t_part, c_part):
+            total = sum_psum.tile([P, BLOCKS, P], F32, tag="total")
+            for b in range(BLOCKS):
+                for k in range(TERMS):
+                    nc.tensor.matmul(
+                        out=total[:, b, :],
+                        lhsT=products[:, k, b * P : (b + 1) * P],
+                        rhs=ident_f32[:],
+                        is_transpose=True,
+                        start=(k == 0),
+                        stop=(k == TERMS - 1),
+                    )
+            h_part = stage.tile([P, BLOCKS, P], F32, tag="h_part")
+            nc.vector.scalar_tensor_tensor(
+                out=h_part[:], in0=t_part[:], scalar=1.0, in1=c_part[:], op0=ALU.subtract, op1=ALU.mult
+            )
+            result = stage.tile([P, BLOCKS, P], F32, tag="result")
+            nc.vector.tensor_tensor(out=result[:], in0=total[:], in1=h_part[:], op=ALU.mult)
+            nc.sync.dma_start(
+                out=out[chunk * CHUNK : (chunk + 1) * CHUNK, group * P : (group + 1) * P].rearrange(
+                    "(b p) i -> p b i", p=P
+                ),
+                in_=result[:],
+            )
+
+        def prepare(group, chunk):
+            if chunk == 0:
+                quantise_wc(group)
+            if group == 0:
+                quantise_grad(chunk)
+            return make_weights(group, chunk)
+
+        steps = [(group, chunk) for group in range(N_GROUPS) for chunk in range(N_CHUNKS)]
+        planes = {0: prepare(*steps[0])}
+        products = {}
+        for s in range(len(steps) + 1):
+            if s + 1 < len(steps):
+                planes[s + 1] = prepare(*steps[s + 1])
+            if s < len(steps):
+                products[s] = multiply(*steps[s], planes[s][0], planes[s][1])
+            if s >= 1:
+                sum_and_store(*steps[s - 1], products[s - 1], planes[s - 1][2], planes[s - 1][3])

@@ -21,6 +21,7 @@ CHUNK = 512
 BLOCKS = CHUNK // P
 N_CHUNKS = TOKENS // CHUNK
 N_GROUPS = FEATURES // P
+FLAT = 3
 X_LIMIT = 8.0
 
 FLOPS = 2 * TOKENS * OUTPUTS * FEATURES * TERMS
@@ -70,12 +71,12 @@ def tile_custombernsteinlayer_kernel(tc, x, weights, coeffs, grad_out, out):
         def load_tokens(chunk):
             rows = slice(chunk * CHUNK, (chunk + 1) * CHUNK)
             blocks = slice(chunk * BLOCKS, (chunk + 1) * BLOCKS)
-            nc.sync.dma_start(out=g_rows[:, blocks, :], in_=grad_out[rows, :].rearrange("(b p) o -> p b o", p=P))
             nc.sync.dma_start(out=x_rows[:, blocks, :], in_=x[rows, :].rearrange("(b p) i -> p b i", p=P))
+            nc.sync.dma_start(out=g_rows[:, blocks, :], in_=grad_out[rows, :].rearrange("(b p) o -> p b o", p=P))
 
+        load_tokens(0)
         nc.sync.dma_start(out=w_rows[:], in_=weights.rearrange("(u p e) i -> p u e i", u=2, e=2))
         coeff_tiles = {0: load_coeffs(0)}
-        load_tokens(0)
         load_tokens(1)
         coeff_tiles[1] = load_coeffs(1)
         load_tokens(2)
@@ -126,8 +127,10 @@ def tile_custombernsteinlayer_kernel(tc, x, weights, coeffs, grad_out, out):
                 )
             cols = slice(chunk * CHUNK, (chunk + 1) * CHUNK)
             nc.vector.quantize_mx(out=g_codes[:, cols].bitcast(E5M2_X4), scales=g_scales[:, cols], in_=gq[:])
+
+        def clamp_x(chunk):
             blocks = slice(chunk * BLOCKS, (chunk + 1) * BLOCKS)
-            nc.gpsimd.tensor_scalar(
+            nc.vector.tensor_scalar(
                 out=x_rows[:, blocks, :], in0=x_rows[:, blocks, :],
                 scalar1=-X_LIMIT, scalar2=X_LIMIT, op0=ALU.max, op1=ALU.min,
             )
@@ -142,14 +145,27 @@ def tile_custombernsteinlayer_kernel(tc, x, weights, coeffs, grad_out, out):
                 )
             e_planes = stage.tile([P, ORDER, CHUNK], F32, tag="e_planes")
             for j in range(ORDER):
-                nc.scalar.activation(
-                    out=e_planes[:, j, :], in_=x_t[:], func=ACT.Exp,
-                    scale=float(2 * j - 6), bias=math.log(binomial(ORDER - 1, j)),
-                )
+                if j != FLAT:
+                    nc.scalar.activation(
+                        out=e_planes[:, j, :], in_=x_t[:], func=ACT.Exp,
+                        scale=float(2 * (j - FLAT)), bias=math.log(binomial(ORDER - 1, j)),
+                    )
             d_planes = stage.tile([P, ORDER - 1, CHUNK], F32, tag="d_planes")
-            for k in range(1, ORDER):
-                nc.gpsimd.tensor_tensor(
-                    out=d_planes[:, k - 1, :], in0=e_planes[:, k - 1, :], in1=e_planes[:, k, :], op=ALU.subtract
+            flat_value = float(binomial(ORDER - 1, FLAT))
+            nc.scalar.activation(
+                out=d_planes[:, FLAT - 1, :], in_=e_planes[:, FLAT - 1, :], func=ACT.Identity,
+                scale=1.0, bias=-flat_value,
+            )
+            nc.scalar.activation(
+                out=d_planes[:, FLAT, :], in_=e_planes[:, FLAT + 1, :], func=ACT.Identity,
+                scale=-1.0, bias=flat_value,
+            )
+            for first, last in ((0, FLAT - 1), (FLAT + 1, ORDER - 1)):
+                nc.vector.tensor_tensor(
+                    out=d_planes[:, first:last, :],
+                    in0=e_planes[:, first:last, :],
+                    in1=e_planes[:, first + 1 : last + 1, :],
+                    op=ALU.subtract,
                 )
             x_part = x_rows[:, chunk * BLOCKS : (chunk + 1) * BLOCKS, group * P : (group + 1) * P]
             t_part = stage.tile([P, BLOCKS, P], F32, tag="t_part", bufs=3)
@@ -212,6 +228,8 @@ def tile_custombernsteinlayer_kernel(tc, x, weights, coeffs, grad_out, out):
             )
 
         def prepare(group, chunk):
+            if group == 0:
+                clamp_x(chunk)
             if chunk == 0:
                 quantise_wc(group)
             if group == 0:

@@ -151,16 +151,24 @@ def tile_custombernsteinlayer_kernel(tc, x, weights, coeffs, grad_out, out):
                         scale=float(2 * (j - FLAT)), bias=math.log(binomial(ORDER - 1, j)),
                     )
             d_planes = stage.tile([P, ORDER - 1, CHUNK], F32, tag="d_planes")
-            flat_value = float(binomial(ORDER - 1, FLAT))
-            nc.scalar.activation(
-                out=d_planes[:, FLAT - 1, :], in_=e_planes[:, FLAT - 1, :], func=ACT.Identity,
-                scale=1.0, bias=-flat_value,
-            )
-            nc.scalar.activation(
-                out=d_planes[:, FLAT, :], in_=e_planes[:, FLAT + 1, :], func=ACT.Identity,
-                scale=-1.0, bias=flat_value,
-            )
-            for first, last in ((0, FLAT - 1), (FLAT + 1, ORDER - 1)):
+            for side in (-1, 1):
+                near = binomial(ORDER - 1, FLAT + side)
+                far = binomial(ORDER - 1, FLAT + 2 * side)
+                flat = binomial(ORDER - 1, FLAT)
+                e_near = e_planes[:, FLAT + side, :]
+                d_near = d_planes[:, FLAT - 1 if side < 0 else FLAT, :]
+                nc.scalar.activation(
+                    out=d_near, in_=e_near, func=ACT.Identity, scale=float(-side), bias=float(side * flat)
+                )
+                d_far = d_planes[:, FLAT - 2 if side < 0 else FLAT + 1, :]
+                root = math.sqrt(far)
+                nc.scalar.activation(
+                    out=d_far, in_=e_near, func=ACT.Square, scale=root / near, bias=-root * near / (2.0 * far)
+                )
+                nc.scalar.activation(
+                    out=d_far, in_=d_far, func=ACT.Identity, scale=float(-side), bias=side * near * near / (4.0 * far)
+                )
+            for first, last in ((0, FLAT - 2), (FLAT + 2, ORDER - 1)):
                 nc.vector.tensor_tensor(
                     out=d_planes[:, first:last, :],
                     in0=e_planes[:, first:last, :],

@@ -23,6 +23,7 @@ N_CHUNKS = TOKENS // CHUNK
 N_GROUPS = FEATURES // P
 FLAT = 3
 X_LIMIT = 8.0
+AHEAD = 2
 
 FLOPS = 2 * TOKENS * OUTPUTS * FEATURES * TERMS
 
@@ -34,6 +35,10 @@ def binomial(n, k):
     return value
 
 
+def gamma(k):
+    return 8.0 / binomial(ORDER, k)
+
+
 def tile_custombernsteinlayer_kernel(tc, x, weights, coeffs, grad_out, out):
     nc = tc.nc
     with ExitStack() as ctx:
@@ -42,6 +47,7 @@ def tile_custombernsteinlayer_kernel(tc, x, weights, coeffs, grad_out, out):
         mx_psum = ctx.enter_context(tc.psum_pool(name="mx_psum", bufs=5))
         tr_psum = ctx.enter_context(tc.psum_pool(name="tr_psum", bufs=2))
         sum_psum = ctx.enter_context(tc.psum_pool(name="sum_psum", bufs=1))
+        ctx.enter_context(tc.manual_schedule())
 
         ident_f32 = keep.tile([P, P], F32)
         make_identity(nc, ident_f32[:])
@@ -50,7 +56,8 @@ def tile_custombernsteinlayer_kernel(tc, x, weights, coeffs, grad_out, out):
 
         x_rows = keep.tile([P, N_CHUNKS * BLOCKS, FEATURES], BF16)
         g_rows = keep.tile([P, N_CHUNKS * BLOCKS, OUTPUTS], BF16)
-        w_rows = keep.tile([P, 2, 2, FEATURES], BF16)
+        w_rows = keep.tile([P, PACK, FEATURES], BF16)
+        w_words = keep.tile([P, FEATURES, PACK], BF16)
         g_codes = keep.tile([P, TOKENS], U32, align_bytes=64)
         g_scales = keep.tile([P, TOKENS], U8, align_bytes=64)
         wc_codes = keep.tile([P, N_GROUPS, TERMS * P], U32, align_bytes=64)
@@ -58,15 +65,16 @@ def tile_custombernsteinlayer_kernel(tc, x, weights, coeffs, grad_out, out):
 
         coeff_view = coeffs.rearrange("(u p e) i k -> p u e (i k)", u=2, e=2)
         group_cols = P * TERMS
+        coeff_tiles = {}
 
         def load_coeffs(group):
-            co = stage.tile([P, 2, 2, group_cols], BF16, tag="co")
+            co = stage.tile([P, PACK, group_cols], BF16, tag="co")
             for u in range(2):
                 nc.sync.dma_start(
-                    out=co[:, u, :, :],
+                    out=co[:, 2 * u : 2 * u + 2, :],
                     in_=coeff_view[:, u, :, group * group_cols : (group + 1) * group_cols],
                 )
-            return co
+            coeff_tiles[group] = co
 
         def load_tokens(chunk):
             rows = slice(chunk * CHUNK, (chunk + 1) * CHUNK)
@@ -74,24 +82,16 @@ def tile_custombernsteinlayer_kernel(tc, x, weights, coeffs, grad_out, out):
             nc.sync.dma_start(out=x_rows[:, blocks, :], in_=x[rows, :].rearrange("(b p) i -> p b i", p=P))
             nc.sync.dma_start(out=g_rows[:, blocks, :], in_=grad_out[rows, :].rearrange("(b p) o -> p b o", p=P))
 
-        load_tokens(0)
-        nc.sync.dma_start(out=w_rows[:], in_=weights.rearrange("(u p e) i -> p u e i", u=2, e=2))
-        coeff_tiles = {0: load_coeffs(0)}
-        load_tokens(1)
-        coeff_tiles[1] = load_coeffs(1)
-        load_tokens(2)
-        load_tokens(3)
-
         def quantise_wc(group):
-            co = coeff_tiles[group]
             wq = stage.tile([P, TERMS, P, PACK], BF16, tag="wq", bufs=1, align_bytes=64)
-            gains = w_rows[:, :, :, group * P : (group + 1) * P].rearrange("p u e i -> p i (u e)")
             nc.vector.tensor_tensor(
                 out=wq[:],
-                in0=co[:].rearrange("p u e (i k) -> p k i (u e)", k=TERMS),
-                in1=gains.unsqueeze(1).to_broadcast([P, TERMS, P, PACK]),
+                in0=coeff_tiles[group][:].rearrange("p t (i k) -> p k i t", k=TERMS),
+                in1=w_words[:, group * P : (group + 1) * P, :].unsqueeze(1).to_broadcast([P, TERMS, P, PACK]),
                 op=ALU.mult,
             )
+            if group + 2 < N_GROUPS:
+                load_coeffs(group + 2)
             flat = wq[:].rearrange("p k i t -> p (k i t)")
             wide = ORDER * P
             nc.vector.quantize_mx(
@@ -104,8 +104,13 @@ def tile_custombernsteinlayer_kernel(tc, x, weights, coeffs, grad_out, out):
                 scales=wc_scales[:, group, wide : wide + P],
                 in_=flat[:, wide * PACK : (wide + P) * PACK],
             )
-            if group + 2 < N_GROUPS:
-                coeff_tiles[group + 2] = load_coeffs(group + 2)
+
+        def clamp_x(chunk):
+            blocks = slice(chunk * BLOCKS, (chunk + 1) * BLOCKS)
+            nc.vector.tensor_scalar(
+                out=x_rows[:, blocks, :], in0=x_rows[:, blocks, :],
+                scalar1=-X_LIMIT, scalar2=X_LIMIT, op0=ALU.max, op1=ALU.min,
+            )
 
         def quantise_grad(chunk):
             g_words = g_rows[:].bitcast(F32)
@@ -128,14 +133,16 @@ def tile_custombernsteinlayer_kernel(tc, x, weights, coeffs, grad_out, out):
             cols = slice(chunk * CHUNK, (chunk + 1) * CHUNK)
             nc.vector.quantize_mx(out=g_codes[:, cols].bitcast(E5M2_X4), scales=g_scales[:, cols], in_=gq[:])
 
-        def clamp_x(chunk):
-            blocks = slice(chunk * BLOCKS, (chunk + 1) * BLOCKS)
-            nc.vector.tensor_scalar(
-                out=x_rows[:, blocks, :], in0=x_rows[:, blocks, :],
-                scalar1=-X_LIMIT, scalar2=X_LIMIT, op0=ALU.max, op1=ALU.min,
-            )
+        def first_use(step):
+            group, chunk = step
+            if group == 0:
+                clamp_x(chunk)
+                quantise_grad(chunk)
+            if chunk == 0:
+                quantise_wc(group)
 
-        def make_weights(group, chunk):
+        def scalar_planes(step):
+            group, chunk = step
             x_t = tr_psum.tile([P, CHUNK], BF16, tag="tr")
             for b in range(BLOCKS):
                 nc.tensor.transpose(
@@ -144,37 +151,48 @@ def tile_custombernsteinlayer_kernel(tc, x, weights, coeffs, grad_out, out):
                     identity=ident_bf16[:],
                 )
             e_planes = stage.tile([P, ORDER, CHUNK], F32, tag="e_planes")
-            for j in range(ORDER):
-                if j != FLAT:
-                    nc.scalar.activation(
-                        out=e_planes[:, j, :], in_=x_t[:], func=ACT.Exp,
-                        scale=float(2 * (j - FLAT)), bias=math.log(binomial(ORDER - 1, j)),
-                    )
-            d_planes = stage.tile([P, ORDER - 1, CHUNK], F32, tag="d_planes")
+            s_planes = stage.tile([P, 2, CHUNK], F32, tag="s_planes")
+            d_planes = stage.tile([P, 3, CHUNK], F32, tag="d_planes")
+
+            def exp_plane(j, gain):
+                nc.scalar.activation(
+                    out=e_planes[:, j, :], in_=x_t[:], func=ACT.Exp, scale=float(2 * (j - FLAT)), bias=math.log(gain)
+                )
+
+            recipe = {
+                0: ("times", e_planes[:, 0, :], gamma(0)),
+                1: ("times", d_planes[:, 0, :], -gamma(1)),
+                ORDER - 2: ("times", d_planes[:, 1, :], -gamma(ORDER - 2)),
+                ORDER - 1: ("times", d_planes[:, 2, :], -gamma(ORDER - 1)),
+                ORDER: ("times", e_planes[:, ORDER - 1, :], -gamma(ORDER)),
+            }
+            exp_plane(0, binomial(ORDER - 1, 0))
+            exp_plane(1, binomial(ORDER - 1, 1))
+            flat = binomial(ORDER - 1, FLAT)
             for side in (-1, 1):
                 near = binomial(ORDER - 1, FLAT + side)
                 far = binomial(ORDER - 1, FLAT + 2 * side)
-                flat = binomial(ORDER - 1, FLAT)
-                e_near = e_planes[:, FLAT + side, :]
-                d_near = d_planes[:, FLAT - 1 if side < 0 else FLAT, :]
+                k_near = FLAT if side < 0 else FLAT + 1
+                k_far = k_near + side
+                middle = near / (2.0 * far)
+                line = e_planes[:, FLAT + side, :]
+                square = s_planes[:, (side + 1) // 2, :]
+                exp_plane(FLAT + side, gamma(k_near) * near)
+                root = math.sqrt(gamma(k_far) * far)
                 nc.scalar.activation(
-                    out=d_near, in_=e_near, func=ACT.Identity, scale=float(-side), bias=float(side * flat)
+                    out=square, in_=line, func=ACT.Square, scale=root / (gamma(k_near) * near), bias=-root * middle
                 )
-                d_far = d_planes[:, FLAT - 2 if side < 0 else FLAT + 1, :]
-                root = math.sqrt(far)
-                nc.scalar.activation(
-                    out=d_far, in_=e_near, func=ACT.Square, scale=root / near, bias=-root * near / (2.0 * far)
-                )
-                nc.scalar.activation(
-                    out=d_far, in_=d_far, func=ACT.Identity, scale=float(-side), bias=side * near * near / (4.0 * far)
-                )
-            for first, last in ((0, FLAT - 2), (FLAT + 2, ORDER - 1)):
-                nc.vector.tensor_tensor(
-                    out=d_planes[:, first:last, :],
-                    in0=e_planes[:, first:last, :],
-                    in1=e_planes[:, first + 1 : last + 1, :],
-                    op=ALU.subtract,
-                )
+                for k, plane, constant in (
+                    (k_near, line, gamma(k_near) * flat),
+                    (k_far, square, gamma(k_far) * near * near / (4.0 * far)),
+                ):
+                    if side > 0:
+                        recipe[k] = ("minus", plane, constant)
+                    else:
+                        nc.scalar.activation(out=plane, in_=plane, func=ACT.Identity, scale=-1.0, bias=constant)
+                        recipe[k] = ("times", plane, 1.0)
+            for j in range(FLAT + 2, ORDER):
+                exp_plane(j, binomial(ORDER - 1, j))
             x_part = x_rows[:, chunk * BLOCKS : (chunk + 1) * BLOCKS, group * P : (group + 1) * P]
             t_part = stage.tile([P, BLOCKS, P], F32, tag="t_part", bufs=3)
             c_part = stage.tile([P, BLOCKS, P], F32, tag="c_part", bufs=3)
@@ -182,9 +200,20 @@ def tile_custombernsteinlayer_kernel(tc, x, weights, coeffs, grad_out, out):
             nc.scalar.activation(out=c_part[:], in_=t_part[:], func=ACT.Square)
             nc.scalar.activation(out=c_part[:], in_=c_part[:], func=ACT.Square, scale=-1.0, bias=1.0)
             nc.scalar.activation(out=c_part[:], in_=c_part[:], func=ACT.Square)
-            return e_planes, d_planes, t_part, c_part
+            return {"e": e_planes, "d": d_planes, "recipe": recipe, "t": t_part, "c": c_part}
 
-        def multiply(group, chunk, e_planes, d_planes):
+        def vector_planes(made):
+            e_planes, d_planes = made["e"], made["d"]
+            nc.vector.tensor_tensor(
+                out=d_planes[:, 0, :], in0=e_planes[:, 0, :], in1=e_planes[:, 1, :], op=ALU.subtract
+            )
+            nc.vector.tensor_tensor(
+                out=d_planes[:, 1:3, :], in0=e_planes[:, ORDER - 3 : ORDER - 1, :],
+                in1=e_planes[:, ORDER - 2 : ORDER, :], op=ALU.subtract,
+            )
+
+        def multiply(step, made):
+            group, chunk = step
             products = stage.tile([P, TERMS, CHUNK], F32, tag="products")
             cols = slice(chunk * CHUNK, (chunk + 1) * CHUNK)
             for k in range(TERMS):
@@ -198,19 +227,19 @@ def tile_custombernsteinlayer_kernel(tc, x, weights, coeffs, grad_out, out):
                     start=True,
                     stop=True,
                 )
-                gamma = -8.0 / binomial(ORDER, k)
-                if k == 0:
-                    plane, factor = e_planes[:, 0, :], -gamma
-                elif k == ORDER:
-                    plane, factor = e_planes[:, ORDER - 1, :], gamma
+                form, plane, number = made["recipe"][k]
+                if form == "times":
+                    nc.vector.scalar_tensor_tensor(
+                        out=products[:, k, :], in0=g_k[:], scalar=number, in1=plane, op0=ALU.mult, op1=ALU.mult
+                    )
                 else:
-                    plane, factor = d_planes[:, k - 1, :], gamma
-                nc.vector.scalar_tensor_tensor(
-                    out=products[:, k, :], in0=g_k[:], scalar=factor, in1=plane, op0=ALU.mult, op1=ALU.mult
-                )
+                    nc.vector.scalar_tensor_tensor(
+                        out=products[:, k, :], in0=plane, scalar=number, in1=g_k[:], op0=ALU.subtract, op1=ALU.mult
+                    )
             return products
 
-        def sum_and_store(group, chunk, products, t_part, c_part):
+        def sum_and_store(step, made, products):
+            group, chunk = step
             total = sum_psum.tile([P, BLOCKS, P], F32, tag="total")
             for b in range(BLOCKS):
                 for k in range(TERMS):
@@ -224,7 +253,7 @@ def tile_custombernsteinlayer_kernel(tc, x, weights, coeffs, grad_out, out):
                     )
             h_part = stage.tile([P, BLOCKS, P], F32, tag="h_part")
             nc.vector.scalar_tensor_tensor(
-                out=h_part[:], in0=t_part[:], scalar=1.0, in1=c_part[:], op0=ALU.subtract, op1=ALU.mult
+                out=h_part[:], in0=made["t"][:], scalar=1.0, in1=made["c"][:], op0=ALU.subtract, op1=ALU.mult
             )
             result = stage.tile([P, BLOCKS, P], F32, tag="result")
             nc.vector.tensor_tensor(out=result[:], in0=total[:], in1=h_part[:], op=ALU.mult)
@@ -235,22 +264,38 @@ def tile_custombernsteinlayer_kernel(tc, x, weights, coeffs, grad_out, out):
                 in_=result[:],
             )
 
-        def prepare(group, chunk):
-            if group == 0:
-                clamp_x(chunk)
-            if chunk == 0:
-                quantise_wc(group)
-            if group == 0:
-                quantise_grad(chunk)
-            return make_weights(group, chunk)
+        nc.sync.dma_start(out=x_rows[:, 0:BLOCKS, :], in_=x[0:CHUNK, :].rearrange("(b p) i -> p b i", p=P))
+        nc.sync.dma_start(
+            out=w_rows[:].rearrange("p (u e) i -> p u e i", u=2), in_=weights.rearrange("(u p e) i -> p u e i", u=2, e=2)
+        )
+        load_coeffs(0)
+        nc.sync.dma_start(out=g_rows[:, 0:BLOCKS, :], in_=grad_out[0:CHUNK, :].rearrange("(b p) o -> p b o", p=P))
+        load_tokens(1)
+        load_coeffs(1)
+        load_tokens(2)
+        load_tokens(3)
 
         steps = [(group, chunk) for group in range(N_GROUPS) for chunk in range(N_CHUNKS)]
-        planes = {0: prepare(*steps[0])}
+        made = {}
         products = {}
+
+        clamp_x(0)
+        made[0] = scalar_planes(steps[0])
+        nc.vector.tensor_copy(out=w_words[:], in_=w_rows[:].rearrange("p t i -> p i t"))
+        quantise_wc(0)
+        quantise_grad(0)
+        vector_planes(made[0])
+        for s in range(1, AHEAD):
+            first_use(steps[s])
+
         for s in range(len(steps) + 1):
             if s + 1 < len(steps):
-                planes[s + 1] = prepare(*steps[s + 1])
+                made[s + 1] = scalar_planes(steps[s + 1])
             if s < len(steps):
-                products[s] = multiply(*steps[s], planes[s][0], planes[s][1])
+                products[s] = multiply(steps[s], made[s])
+            if s + 1 < len(steps):
+                vector_planes(made[s + 1])
+            if s + AHEAD < len(steps):
+                first_use(steps[s + AHEAD])
             if s >= 1:
-                sum_and_store(*steps[s - 1], products[s - 1], planes[s - 1][2], planes[s - 1][3])
+                sum_and_store(steps[s - 1], made[s - 1], products[s - 1])

@@ -47,7 +47,6 @@ def tile_custombernsteinlayer_kernel(tc, x, weights, coeffs, grad_out, out):
         mx_psum = ctx.enter_context(tc.psum_pool(name="mx_psum", bufs=5))
         tr_psum = ctx.enter_context(tc.psum_pool(name="tr_psum", bufs=2))
         sum_psum = ctx.enter_context(tc.psum_pool(name="sum_psum", bufs=1))
-        ctx.enter_context(tc.manual_schedule())
 
         ident_f32 = keep.tile([P, P], F32)
         make_identity(nc, ident_f32[:])
@@ -84,14 +83,19 @@ def tile_custombernsteinlayer_kernel(tc, x, weights, coeffs, grad_out, out):
 
         def quantise_wc(group):
             wq = stage.tile([P, TERMS, P, PACK], BF16, tag="wq", bufs=1, align_bytes=64)
+            by_plane = coeff_tiles[group][:].rearrange("p t (i k) -> p k i t", k=TERMS)
+            for k in range(TERMS):
+                nc.gpsimd.tensor_scalar(
+                    out=wq[:, k, :, :], in0=by_plane[:, k, :, :], scalar1=1.0, scalar2=0.0, op0=ALU.mult, op1=ALU.add
+                )
+            if group + 2 < N_GROUPS:
+                load_coeffs(group + 2)
             nc.vector.tensor_tensor(
                 out=wq[:],
-                in0=coeff_tiles[group][:].rearrange("p t (i k) -> p k i t", k=TERMS),
+                in0=wq[:],
                 in1=w_words[:, group * P : (group + 1) * P, :].unsqueeze(1).to_broadcast([P, TERMS, P, PACK]),
                 op=ALU.mult,
             )
-            if group + 2 < N_GROUPS:
-                load_coeffs(group + 2)
             flat = wq[:].rearrange("p k i t -> p (k i t)")
             wide = ORDER * P
             nc.vector.quantize_mx(
@@ -264,12 +268,11 @@ def tile_custombernsteinlayer_kernel(tc, x, weights, coeffs, grad_out, out):
                 in_=result[:],
             )
 
-        nc.sync.dma_start(out=x_rows[:, 0:BLOCKS, :], in_=x[0:CHUNK, :].rearrange("(b p) i -> p b i", p=P))
+        load_coeffs(0)
         nc.sync.dma_start(
             out=w_rows[:].rearrange("p (u e) i -> p u e i", u=2), in_=weights.rearrange("(u p e) i -> p u e i", u=2, e=2)
         )
-        load_coeffs(0)
-        nc.sync.dma_start(out=g_rows[:, 0:BLOCKS, :], in_=grad_out[0:CHUNK, :].rearrange("(b p) o -> p b o", p=P))
+        load_tokens(0)
         load_tokens(1)
         load_coeffs(1)
         load_tokens(2)

@@ -193,7 +193,9 @@ def tile_custombernsteinlayer_kernel(tc, x, weights, coeffs, grad_out, out):
                     if side > 0:
                         recipe[k] = ("minus", plane, constant)
                     else:
-                        nc.scalar.activation(out=plane, in_=plane, func=ACT.Identity, scale=-1.0, bias=constant)
+                        nc.gpsimd.tensor_scalar(
+                            out=plane, in0=plane, scalar1=-1.0, scalar2=constant, op0=ALU.mult, op1=ALU.add
+                        )
                         recipe[k] = ("times", plane, 1.0)
             for j in range(FLAT + 2, ORDER):
                 exp_plane(j, binomial(ORDER - 1, j))

@@ -18,9 +18,9 @@ PACK = 4
 TOKENS, FEATURES, OUTPUTS, ORDER = 2048, 512, 512, 8
 TERMS = ORDER + 1
 CHUNK = 512
-BLOCKS = CHUNK // P
+STRIPS = CHUNK // P
 N_CHUNKS = TOKENS // CHUNK
-N_GROUPS = FEATURES // P
+N_BANDS = FEATURES // P
 FLAT = 3
 X_LIMIT = 8.0
 AHEAD = 2
@@ -53,66 +53,65 @@ def tile_custombernsteinlayer_kernel(tc, x, weights, coeffs, grad_out, out):
         ident_bf16 = keep.tile([P, P], BF16)
         make_identity(nc, ident_bf16[:])
 
-        x_rows = keep.tile([P, N_CHUNKS * BLOCKS, FEATURES], BF16)
-        g_rows = keep.tile([P, N_CHUNKS * BLOCKS, OUTPUTS], BF16)
+        x_rows = keep.tile([P, N_CHUNKS * STRIPS, FEATURES], BF16)
+        g_rows = keep.tile([P, N_CHUNKS * STRIPS, OUTPUTS], BF16)
         w_rows = keep.tile([P, PACK, FEATURES], BF16)
         w_words = keep.tile([P, FEATURES, PACK], BF16)
         g_codes = keep.tile([P, TOKENS], U32, align_bytes=64)
         g_scales = keep.tile([P, TOKENS], U8, align_bytes=64)
-        wc_codes = keep.tile([P, N_GROUPS, TERMS * P], U32, align_bytes=64)
-        wc_scales = keep.tile([P, N_GROUPS, TERMS * P], U8, align_bytes=64)
+        wc_codes = keep.tile([P, N_BANDS, TERMS * P], U32, align_bytes=64)
+        wc_scales = keep.tile([P, N_BANDS, TERMS * P], U8, align_bytes=64)
 
         coeff_view = coeffs.rearrange("(u p e) i k -> p u e (i k)", u=2, e=2)
-        group_cols = P * TERMS
+        band_cols = P * TERMS
         coeff_tiles = {}
 
-        def load_coeffs(group):
-            co = stage.tile([P, PACK, group_cols], BF16, tag="co")
+        def load_coeffs(band):
+            co = stage.tile([P, PACK, band_cols], BF16, tag="co")
             for u in range(2):
                 nc.sync.dma_start(
                     out=co[:, 2 * u : 2 * u + 2, :],
-                    in_=coeff_view[:, u, :, group * group_cols : (group + 1) * group_cols],
+                    in_=coeff_view[:, u, :, band * band_cols : (band + 1) * band_cols],
                 )
-            coeff_tiles[group] = co
+            coeff_tiles[band] = co
 
-        def load_tokens(chunk):
-            rows = slice(chunk * CHUNK, (chunk + 1) * CHUNK)
-            blocks = slice(chunk * BLOCKS, (chunk + 1) * BLOCKS)
-            nc.sync.dma_start(out=x_rows[:, blocks, :], in_=x[rows, :].rearrange("(b p) i -> p b i", p=P))
-            nc.sync.dma_start(out=g_rows[:, blocks, :], in_=grad_out[rows, :].rearrange("(b p) o -> p b o", p=P))
+        def load_x(chunk):
+            nc.sync.dma_start(
+                out=x_rows[:, chunk * STRIPS : (chunk + 1) * STRIPS, :],
+                in_=x[chunk * CHUNK : (chunk + 1) * CHUNK, :].rearrange("(s p) i -> p s i", p=P),
+            )
 
-        def quantise_wc(group):
+        def load_grad(chunk):
+            nc.sync.dma_start(
+                out=g_rows[:, chunk * STRIPS : (chunk + 1) * STRIPS, :],
+                in_=grad_out[chunk * CHUNK : (chunk + 1) * CHUNK, :].rearrange("(s p) o -> p s o", p=P),
+            )
+
+        def quantise_wc(band):
             wq = stage.tile([P, TERMS, P, PACK], BF16, tag="wq", bufs=1, align_bytes=64)
-            by_plane = coeff_tiles[group][:].rearrange("p t (i k) -> p k i t", k=TERMS)
-            for k in range(TERMS):
-                nc.gpsimd.tensor_scalar(
-                    out=wq[:, k, :, :], in0=by_plane[:, k, :, :], scalar1=1.0, scalar2=0.0, op0=ALU.mult, op1=ALU.add
+            by_plane = coeff_tiles[band][:].rearrange("p t (i k) -> p k i t", k=TERMS)
+            gains = w_words[:, band * P : (band + 1) * P, :].unsqueeze(1)
+            for first, count in ((0, 4), (4, 4), (8, 1)):
+                for k in range(first, first + count):
+                    nc.gpsimd.tensor_scalar(
+                        out=wq[:, k, :, :], in0=by_plane[:, k, :, :],
+                        scalar1=1.0, scalar2=0.0, op0=ALU.mult, op1=ALU.add,
+                    )
+                part = wq[:, first : first + count, :, :]
+                nc.vector.tensor_tensor(out=part, in0=part, in1=gains.to_broadcast([P, count, P, PACK]), op=ALU.mult)
+                cols = slice(first * P, (first + count) * P)
+                nc.vector.quantize_mx(
+                    out=wc_codes[:, band, cols].bitcast(E4M3_X4),
+                    scales=wc_scales[:, band, cols],
+                    in_=part.rearrange("p k i t -> p (k i t)"),
                 )
-            if group + 2 < N_GROUPS:
-                load_coeffs(group + 2)
-            nc.vector.tensor_tensor(
-                out=wq[:],
-                in0=wq[:],
-                in1=w_words[:, group * P : (group + 1) * P, :].unsqueeze(1).to_broadcast([P, TERMS, P, PACK]),
-                op=ALU.mult,
-            )
-            flat = wq[:].rearrange("p k i t -> p (k i t)")
-            wide = ORDER * P
-            nc.vector.quantize_mx(
-                out=wc_codes[:, group, 0:wide].bitcast(E4M3_X4),
-                scales=wc_scales[:, group, 0:wide],
-                in_=flat[:, 0 : wide * PACK],
-            )
-            nc.vector.quantize_mx(
-                out=wc_codes[:, group, wide : wide + P].bitcast(E4M3_X4),
-                scales=wc_scales[:, group, wide : wide + P],
-                in_=flat[:, wide * PACK : (wide + P) * PACK],
-            )
+            if band + 2 < N_BANDS:
+                load_coeffs(band + 2)
 
         def clamp_x(chunk):
-            blocks = slice(chunk * BLOCKS, (chunk + 1) * BLOCKS)
+            strips = slice(chunk * STRIPS, (chunk + 1) * STRIPS)
             nc.vector.tensor_scalar(
-                out=x_rows[:, blocks, :], in0=x_rows[:, blocks, :],
+                out=x_rows[:, strips, :], in0=x_rows[:, strips, :],
                 scalar1=-X_LIMIT, scalar2=X_LIMIT, op0=ALU.max, op1=ALU.min,
             )
 
@@ -122,12 +121,12 @@ def tile_custombernsteinlayer_kernel(tc, x, weights, coeffs, grad_out, out):
             gq_words = gq[:].bitcast(F32).rearrange("p (n u) -> p n u", u=2)
             for half in range(2):
                 g_t = tr_psum.tile([P, 2, 2 * P], F32, tag="tr")
-                for b in range(2):
-                    block = chunk * BLOCKS + 2 * half + b
+                for s in range(2):
+                    strip = chunk * STRIPS + 2 * half + s
                     for u in range(2):
                         nc.tensor.transpose(
-                            out=g_t[:, u, b * P : (b + 1) * P],
-                            in_=g_words[:, block, u * P : (u + 1) * P],
+                            out=g_t[:, u, s * P : (s + 1) * P],
+                            in_=g_words[:, strip, u * P : (u + 1) * P],
                             identity=ident_f32[:],
                         )
                 nc.scalar.copy(
@@ -138,20 +137,20 @@ def tile_custombernsteinlayer_kernel(tc, x, weights, coeffs, grad_out, out):
             nc.vector.quantize_mx(out=g_codes[:, cols].bitcast(E5M2_X4), scales=g_scales[:, cols], in_=gq[:])
 
         def first_use(step):
-            group, chunk = step
-            if group == 0:
+            band, chunk = step
+            if band == 0:
                 clamp_x(chunk)
                 quantise_grad(chunk)
             if chunk == 0:
-                quantise_wc(group)
+                quantise_wc(band)
 
         def scalar_planes(step):
-            group, chunk = step
+            band, chunk = step
             x_t = tr_psum.tile([P, CHUNK], BF16, tag="tr")
-            for b in range(BLOCKS):
+            for s in range(STRIPS):
                 nc.tensor.transpose(
-                    out=x_t[:, b * P : (b + 1) * P],
-                    in_=x_rows[:, chunk * BLOCKS + b, group * P : (group + 1) * P],
+                    out=x_t[:, s * P : (s + 1) * P],
+                    in_=x_rows[:, chunk * STRIPS + s, band * P : (band + 1) * P],
                     identity=ident_bf16[:],
                 )
             e_planes = stage.tile([P, ORDER, CHUNK], F32, tag="e_planes")
@@ -193,15 +192,13 @@ def tile_custombernsteinlayer_kernel(tc, x, weights, coeffs, grad_out, out):
                     if side > 0:
                         recipe[k] = ("minus", plane, constant)
                     else:
-                        nc.gpsimd.tensor_scalar(
-                            out=plane, in0=plane, scalar1=-1.0, scalar2=constant, op0=ALU.mult, op1=ALU.add
-                        )
+                        nc.scalar.activation(out=plane, in_=plane, func=ACT.Identity, scale=-1.0, bias=constant)
                         recipe[k] = ("times", plane, 1.0)
             for j in range(FLAT + 2, ORDER):
                 exp_plane(j, binomial(ORDER - 1, j))
-            x_part = x_rows[:, chunk * BLOCKS : (chunk + 1) * BLOCKS, group * P : (group + 1) * P]
-            t_part = stage.tile([P, BLOCKS, P], F32, tag="t_part", bufs=3)
-            c_part = stage.tile([P, BLOCKS, P], F32, tag="c_part", bufs=3)
+            x_part = x_rows[:, chunk * STRIPS : (chunk + 1) * STRIPS, band * P : (band + 1) * P]
+            t_part = stage.tile([P, STRIPS, P], F32, tag="t_part")
+            c_part = stage.tile([P, STRIPS, P], F32, tag="c_part")
             nc.scalar.activation(out=t_part[:], in_=x_part, func=ACT.Tanh)
             nc.scalar.activation(out=c_part[:], in_=t_part[:], func=ACT.Square)
             nc.scalar.activation(out=c_part[:], in_=c_part[:], func=ACT.Square, scale=-1.0, bias=1.0)
@@ -218,16 +215,17 @@ def tile_custombernsteinlayer_kernel(tc, x, weights, coeffs, grad_out, out):
                 in1=e_planes[:, ORDER - 2 : ORDER, :], op=ALU.subtract,
             )
 
-        def multiply(step, made):
-            group, chunk = step
+        def multiply_and_sum(step, made):
+            band, chunk = step
             products = stage.tile([P, TERMS, CHUNK], F32, tag="products")
+            total = sum_psum.tile([P, STRIPS, P], F32, tag="total")
             cols = slice(chunk * CHUNK, (chunk + 1) * CHUNK)
             for k in range(TERMS):
                 g_k = mx_psum.tile([P, CHUNK], F32, tag="g_k")
                 nc.tensor.matmul_mx(
                     out=g_k[:],
-                    lhsT=wc_codes[:, group, k * P : (k + 1) * P].bitcast(E4M3_X4),
-                    lhsT_scale=wc_scales[:, group, k * P : (k + 1) * P],
+                    lhsT=wc_codes[:, band, k * P : (k + 1) * P].bitcast(E4M3_X4),
+                    lhsT_scale=wc_scales[:, band, k * P : (k + 1) * P],
                     rhs=g_codes[:, cols].bitcast(E5M2_X4),
                     rhs_scale=g_scales[:, cols],
                     start=True,
@@ -242,47 +240,47 @@ def tile_custombernsteinlayer_kernel(tc, x, weights, coeffs, grad_out, out):
                     nc.vector.scalar_tensor_tensor(
                         out=products[:, k, :], in0=plane, scalar=number, in1=g_k[:], op0=ALU.subtract, op1=ALU.mult
                     )
-            return products
-
-        def sum_and_store(step, made, products):
-            group, chunk = step
-            total = sum_psum.tile([P, BLOCKS, P], F32, tag="total")
-            for b in range(BLOCKS):
-                for k in range(TERMS):
+                for s in range(STRIPS):
                     nc.tensor.matmul(
-                        out=total[:, b, :],
-                        lhsT=products[:, k, b * P : (b + 1) * P],
+                        out=total[:, s, :],
+                        lhsT=products[:, k, s * P : (s + 1) * P],
                         rhs=ident_f32[:],
                         is_transpose=True,
-                        start=(k == 0),
-                        stop=(k == TERMS - 1),
+                        start=(k == 0 and s == 0),
+                        stop=(k == TERMS - 1 and s == STRIPS - 1),
                     )
-            h_part = stage.tile([P, BLOCKS, P], F32, tag="h_part")
+            return total
+
+        def scale_and_store(step, made, total):
+            band, chunk = step
+            h_part = stage.tile([P, STRIPS, P], F32, tag="h_part")
             nc.vector.scalar_tensor_tensor(
                 out=h_part[:], in0=made["t"][:], scalar=1.0, in1=made["c"][:], op0=ALU.subtract, op1=ALU.mult
             )
-            result = stage.tile([P, BLOCKS, P], F32, tag="result")
+            result = stage.tile([P, STRIPS, P], F32, tag="result")
             nc.vector.tensor_tensor(out=result[:], in0=total[:], in1=h_part[:], op=ALU.mult)
             nc.sync.dma_start(
-                out=out[chunk * CHUNK : (chunk + 1) * CHUNK, group * P : (group + 1) * P].rearrange(
-                    "(b p) i -> p b i", p=P
+                out=out[chunk * CHUNK : (chunk + 1) * CHUNK, band * P : (band + 1) * P].rearrange(
+                    "(s p) i -> p s i", p=P
                 ),
                 in_=result[:],
             )
 
+        load_x(0)
         load_coeffs(0)
         nc.sync.dma_start(
             out=w_rows[:].rearrange("p (u e) i -> p u e i", u=2), in_=weights.rearrange("(u p e) i -> p u e i", u=2, e=2)
         )
-        load_tokens(0)
-        load_tokens(1)
+        load_grad(0)
+        load_x(1)
+        load_grad(1)
         load_coeffs(1)
-        load_tokens(2)
-        load_tokens(3)
+        for chunk in range(2, N_CHUNKS):
+            load_x(chunk)
+            load_grad(chunk)
 
-        steps = [(group, chunk) for group in range(N_GROUPS) for chunk in range(N_CHUNKS)]
+        steps = [(band, chunk) for band in range(N_BANDS) for chunk in range(N_CHUNKS)]
         made = {}
-        products = {}
 
         clamp_x(0)
         made[0] = scalar_planes(steps[0])
@@ -293,14 +291,12 @@ def tile_custombernsteinlayer_kernel(tc, x, weights, coeffs, grad_out, out):
         for s in range(1, AHEAD):
             first_use(steps[s])
 
-        for s in range(len(steps) + 1):
+        for s in range(len(steps)):
             if s + 1 < len(steps):
                 made[s + 1] = scalar_planes(steps[s + 1])
-            if s < len(steps):
-                products[s] = multiply(steps[s], made[s])
+            total = multiply_and_sum(steps[s], made[s])
             if s + 1 < len(steps):
                 vector_planes(made[s + 1])
             if s + AHEAD < len(steps):
                 first_use(steps[s + AHEAD])
-            if s >= 1:
-                sum_and_store(steps[s - 1], made[s - 1], products[s - 1])
+            scale_and_store(steps[s], made[s], total)

import math
from contextlib import ExitStack

import concourse.mybir as mybir
from concourse.masks import make_identity

F32 = mybir.dt.float32
BF16 = mybir.dt.bfloat16
U32 = mybir.dt.uint32
U8 = mybir.dt.uint8
E4M3_X4 = mybir.dt.float8_e4m3fn_x4
E5M2_X4 = mybir.dt.float8_e5m2_x4
ALU = mybir.AluOpType
ACT = mybir.ActivationFunctionType

P = 128
PACK = 4
TOKENS, FEATURES, OUTPUTS, ORDER = 2048, 512, 512, 8
TERMS = ORDER + 1
CHUNK = 512
STRIPS = CHUNK // P
N_CHUNKS = TOKENS // CHUNK
N_BANDS = FEATURES // P
FLAT = 3
X_LIMIT = 8.0
AHEAD = 2

FLOPS = 2 * TOKENS * OUTPUTS * FEATURES * TERMS


def binomial(n, k):
    value = 1
    for j in range(k):
        value = value * (n - j) // (j + 1)
    return value


def gamma(k):
    return 8.0 / binomial(ORDER, k)


def tile_custombernsteinlayer_kernel(tc, x, weights, coeffs, grad_out, out):
    nc = tc.nc
    with ExitStack() as ctx:
        keep = ctx.enter_context(tc.tile_pool(name="keep", bufs=1))
        stage = ctx.enter_context(tc.tile_pool(name="stage", bufs=2))
        mx_psum = ctx.enter_context(tc.psum_pool(name="mx_psum", bufs=5))
        tr_psum = ctx.enter_context(tc.psum_pool(name="tr_psum", bufs=2))
        sum_psum = ctx.enter_context(tc.psum_pool(name="sum_psum", bufs=1))

        ident_f32 = keep.tile([P, P], F32)
        make_identity(nc, ident_f32[:])
        ident_bf16 = keep.tile([P, P], BF16)
        make_identity(nc, ident_bf16[:])

        x_rows = keep.tile([P, N_CHUNKS * STRIPS, FEATURES], BF16)
        g_rows = keep.tile([P, N_CHUNKS * STRIPS, OUTPUTS], BF16)
        w_rows = keep.tile([P, PACK, FEATURES], BF16)
        w_words = keep.tile([P, FEATURES, PACK], BF16)
        g_codes = keep.tile([P, TOKENS], U32, align_bytes=64)
        g_scales = keep.tile([P, TOKENS], U8, align_bytes=64)
        wc_codes = keep.tile([P, N_BANDS, TERMS * P], U32, align_bytes=64)
        wc_scales = keep.tile([P, N_BANDS, TERMS * P], U8, align_bytes=64)

        coeff_view = coeffs.rearrange("(u p e) i k -> p u e (i k)", u=2, e=2)
        band_cols = P * TERMS
        coeff_tiles = {}

        def load_coeffs(band):
            co = stage.tile([P, PACK, band_cols], BF16, tag="co")
            for u in range(2):
                nc.sync.dma_start(
                    out=co[:, 2 * u : 2 * u + 2, :],
                    in_=coeff_view[:, u, :, band * band_cols : (band + 1) * band_cols],
                )
            coeff_tiles[band] = co

        def load_x(chunk):
            nc.sync.dma_start(
                out=x_rows[:, chunk * STRIPS : (chunk + 1) * STRIPS, :],
                in_=x[chunk * CHUNK : (chunk + 1) * CHUNK, :].rearrange("(s p) i -> p s i", p=P),
            )

        def load_grad(chunk):
            nc.sync.dma_start(
                out=g_rows[:, chunk * STRIPS : (chunk + 1) * STRIPS, :],
                in_=grad_out[chunk * CHUNK : (chunk + 1) * CHUNK, :].rearrange("(s p) o -> p s o", p=P),
            )

        def quantise_wc(band):
            wq = stage.tile([P, TERMS, P, PACK], BF16, tag="wq", bufs=1, align_bytes=64)
            by_plane = coeff_tiles[band][:].rearrange("p t (i k) -> p k i t", k=TERMS)
            gains = w_words[:, band * P : (band + 1) * P, :].unsqueeze(1)
            for first, count in ((0, 4), (4, 4), (8, 1)):
                for k in range(first, first + count):
                    nc.gpsimd.tensor_scalar(
                        out=wq[:, k, :, :], in0=by_plane[:, k, :, :],
                        scalar1=1.0, scalar2=0.0, op0=ALU.mult, op1=ALU.add,
                    )
                part = wq[:, first : first + count, :, :]
                nc.vector.tensor_tensor(out=part, in0=part, in1=gains.to_broadcast([P, count, P, PACK]), op=ALU.mult)
                cols = slice(first * P, (first + count) * P)
                nc.vector.quantize_mx(
                    out=wc_codes[:, band, cols].bitcast(E4M3_X4),
                    scales=wc_scales[:, band, cols],
                    in_=part.rearrange("p k i t -> p (k i t)"),
                )
            if band + 2 < N_BANDS:
                load_coeffs(band + 2)

        def clamp_x(chunk):
            strips = slice(chunk * STRIPS, (chunk + 1) * STRIPS)
            nc.vector.tensor_scalar(
                out=x_rows[:, strips, :], in0=x_rows[:, strips, :],
                scalar1=-X_LIMIT, scalar2=X_LIMIT, op0=ALU.max, op1=ALU.min,
            )

        def quantise_grad(chunk):
            g_words = g_rows[:].bitcast(F32)
            gq = stage.tile([P, CHUNK * PACK], BF16, tag="gq", align_bytes=64)
            gq_words = gq[:].bitcast(F32).rearrange("p (n u) -> p n u", u=2)
            for half in range(2):
                g_t = tr_psum.tile([P, 2, 2 * P], F32, tag="tr")
                for s in range(2):
                    strip = chunk * STRIPS + 2 * half + s
                    for u in range(2):
                        nc.tensor.transpose(
                            out=g_t[:, u, s * P : (s + 1) * P],
                            in_=g_words[:, strip, u * P : (u + 1) * P],
                            identity=ident_f32[:],
                        )
                nc.scalar.copy(
                    out=gq_words[:, half * 2 * P : (half + 1) * 2 * P, :],
                    in_=g_t[:].rearrange("p u n -> p n u"),
                )
            cols = slice(chunk * CHUNK, (chunk + 1) * CHUNK)
            nc.vector.quantize_mx(out=g_codes[:, cols].bitcast(E5M2_X4), scales=g_scales[:, cols], in_=gq[:])

        def first_use(step):
            band, chunk = step
            if band == 0:
                clamp_x(chunk)
                quantise_grad(chunk)
            if chunk == 0:
                quantise_wc(band)

        def scalar_planes(step):
            band, chunk = step
            x_t = tr_psum.tile([P, CHUNK], BF16, tag="tr")
            for s in range(STRIPS):
                nc.tensor.transpose(
                    out=x_t[:, s * P : (s + 1) * P],
                    in_=x_rows[:, chunk * STRIPS + s, band * P : (band + 1) * P],
                    identity=ident_bf16[:],
                )
            e_planes = stage.tile([P, ORDER, CHUNK], F32, tag="e_planes")
            s_planes = stage.tile([P, 2, CHUNK], F32, tag="s_planes")
            d_planes = stage.tile([P, 3, CHUNK], F32, tag="d_planes")

            def exp_plane(j, gain):
                nc.scalar.activation(
                    out=e_planes[:, j, :], in_=x_t[:], func=ACT.Exp, scale=float(2 * (j - FLAT)), bias=math.log(gain)
                )

            recipe = {
                0: ("times", e_planes[:, 0, :], gamma(0)),
                1: ("times", d_planes[:, 0, :], -gamma(1)),
                ORDER - 2: ("times", d_planes[:, 1, :], -gamma(ORDER - 2)),
                ORDER - 1: ("times", d_planes[:, 2, :], -gamma(ORDER - 1)),
                ORDER: ("times", e_planes[:, ORDER - 1, :], -gamma(ORDER)),
            }
            exp_plane(0, binomial(ORDER - 1, 0))
            exp_plane(1, binomial(ORDER - 1, 1))
            flat = binomial(ORDER - 1, FLAT)
            for side in (-1, 1):
                near = binomial(ORDER - 1, FLAT + side)
                far = binomial(ORDER - 1, FLAT + 2 * side)
                k_near = FLAT if side < 0 else FLAT + 1
                k_far = k_near + side
                middle = near / (2.0 * far)
                line = e_planes[:, FLAT + side, :]
                square = s_planes[:, (side + 1) // 2, :]
                exp_plane(FLAT + side, gamma(k_near) * near)
                root = math.sqrt(gamma(k_far) * far)
                nc.scalar.activation(
                    out=square, in_=line, func=ACT.Square, scale=root / (gamma(k_near) * near), bias=-root * middle
                )
                for k, plane, constant in (
                    (k_near, line, gamma(k_near) * flat),
                    (k_far, square, gamma(k_far) * near * near / (4.0 * far)),
                ):
                    if side > 0:
                        recipe[k] = ("minus", plane, constant)
                    else:
                        nc.scalar.activation(out=plane, in_=plane, func=ACT.Identity, scale=-1.0, bias=constant)
                        recipe[k] = ("times", plane, 1.0)
            for j in range(FLAT + 2, ORDER):
                exp_plane(j, binomial(ORDER - 1, j))
            x_part = x_rows[:, chunk * STRIPS : (chunk + 1) * STRIPS, band * P : (band + 1) * P]
            t_part = stage.tile([P, STRIPS, P], F32, tag="t_part")
            c_part = stage.tile([P, STRIPS, P], F32, tag="c_part")
            nc.scalar.activation(out=t_part[:], in_=x_part, func=ACT.Tanh)
            nc.scalar.activation(out=c_part[:], in_=t_part[:], func=ACT.Square)
            nc.scalar.activation(out=c_part[:], in_=c_part[:], func=ACT.Square, scale=-1.0, bias=1.0)
            nc.scalar.activation(out=c_part[:], in_=c_part[:], func=ACT.Square)
            return {"e": e_planes, "d": d_planes, "recipe": recipe, "t": t_part, "c": c_part}

        def vector_planes(made):
            e_planes, d_planes = made["e"], made["d"]
            nc.vector.tensor_tensor(
                out=d_planes[:, 0, :], in0=e_planes[:, 0, :], in1=e_planes[:, 1, :], op=ALU.subtract
            )
            nc.vector.tensor_tensor(
                out=d_planes[:, 1:3, :], in0=e_planes[:, ORDER - 3 : ORDER - 1, :],
                in1=e_planes[:, ORDER - 2 : ORDER, :], op=ALU.subtract,
            )

        def multiply_and_sum(step, made):
            band, chunk = step
            products = stage.tile([P, TERMS, CHUNK], F32, tag="products")
            total = sum_psum.tile([P, STRIPS, P], F32, tag="total")
            cols = slice(chunk * CHUNK, (chunk + 1) * CHUNK)
            for k in range(TERMS):
                g_k = mx_psum.tile([P, CHUNK], F32, tag="g_k")
                nc.tensor.matmul_mx(
                    out=g_k[:],
                    lhsT=wc_codes[:, band, k * P : (k + 1) * P].bitcast(E4M3_X4),
                    lhsT_scale=wc_scales[:, band, k * P : (k + 1) * P],
                    rhs=g_codes[:, cols].bitcast(E5M2_X4),
                    rhs_scale=g_scales[:, cols],
                    start=True,
                    stop=True,
                )
                form, plane, number = made["recipe"][k]
                if form == "times":
                    nc.vector.scalar_tensor_tensor(
                        out=products[:, k, :], in0=g_k[:], scalar=number, in1=plane, op0=ALU.mult, op1=ALU.mult
                    )
                else:
                    nc.vector.scalar_tensor_tensor(
                        out=products[:, k, :], in0=plane, scalar=number, in1=g_k[:], op0=ALU.subtract, op1=ALU.mult
                    )
                for s in range(STRIPS):
                    nc.tensor.matmul(
                        out=total[:, s, :],
                        lhsT=products[:, k, s * P : (s + 1) * P],
                        rhs=ident_f32[:],
                        is_transpose=True,
                        start=(k == 0 and s == 0),
                        stop=(k == TERMS - 1 and s == STRIPS - 1),
                    )
            return total

        def scale_and_store(step, made, total):
            band, chunk = step
            h_part = stage.tile([P, STRIPS, P], F32, tag="h_part")
            nc.vector.scalar_tensor_tensor(
                out=h_part[:], in0=made["t"][:], scalar=1.0, in1=made["c"][:], op0=ALU.subtract, op1=ALU.mult
            )
            result = stage.tile([P, STRIPS, P], F32, tag="result")
            nc.vector.tensor_tensor(out=result[:], in0=total[:], in1=h_part[:], op=ALU.mult)
            nc.sync.dma_start(
                out=out[chunk * CHUNK : (chunk + 1) * CHUNK, band * P : (band + 1) * P].rearrange(
                    "(s p) i -> p s i", p=P
                ),
                in_=result[:],
            )

        load_x(0)
        load_coeffs(0)
        nc.sync.dma_start(
            out=w_rows[:].rearrange("p (u e) i -> p u e i", u=2), in_=weights.rearrange("(u p e) i -> p u e i", u=2, e=2)
        )
        load_grad(0)
        load_x(1)
        load_grad(1)
        load_coeffs(1)
        for chunk in range(2, N_CHUNKS):
            load_x(chunk)
            load_grad(chunk)

        steps = [(band, chunk) for band in range(N_BANDS) for chunk in range(N_CHUNKS)]
        made = {}

        clamp_x(0)
        made[0] = scalar_planes(steps[0])
        nc.vector.tensor_copy(out=w_words[:], in_=w_rows[:].rearrange("p t i -> p i t"))
        quantise_wc(0)
        quantise_grad(0)
        vector_planes(made[0])
        for s in range(1, AHEAD):
            first_use(steps[s])

        for s in range(len(steps)):
            if s + 1 < len(steps):
                made[s + 1] = scalar_planes(steps[s + 1])
            total = multiply_and_sum(steps[s], made[s])
            if s + 1 < len(steps):
                vector_planes(made[s + 1])
            if s + AHEAD < len(steps):
                first_use(steps[s + AHEAD])
            scale_and_store(steps[s], made[s], total)
